import numpy as np
import ml_dtypes


def mxq(x, axis, fmt="e4m3"):
    dtype, down = {"e4m3": (ml_dtypes.float8_e4m3fn, 7), "e5m2": (ml_dtypes.float8_e5m2, 14)}[fmt]
    v = np.moveaxis(np.asarray(x, np.float32).astype(ml_dtypes.bfloat16).astype(np.float64), axis, -1)
    blocks = v.reshape(v.shape[:-1] + (-1, 32))
    amax = np.abs(blocks).max(-1, keepdims=True)
    byte = np.maximum(np.where(amax > 0, np.frexp(amax)[1] - 1 + 127, 0) - down, 1)
    scale = np.exp2(byte - 127.0)
    codes = (blocks / scale).astype(np.float32).astype(dtype).astype(np.float64)
    return np.moveaxis((codes * scale).reshape(v.shape), -1, axis)


WIDE = False


def mx_kscale(k):
    if not WIDE:
        return np.ones(k)
    levels = np.array([10, -10, 5, -5, 0])
    if k % 512:
        return np.exp2(np.random.permutation(np.resize(levels, k // 32))).repeat(32)
    a = np.empty((k // 512, 16))
    for p in range(k // 512):
        a[p, :8] = np.random.permutation(np.resize(levels, 8))
        for g in range(8):
            far = levels[np.abs(levels - a[p, g]) >= 10]
            a[p, g + 8] = far[np.random.randint(len(far))]
    return np.exp2(a.ravel()).repeat(32)


BF16 = ml_dtypes.bfloat16


def bf(x):
    return np.asarray(x, np.float32).astype(BF16)


def f64(x):
    return np.asarray(x).astype(np.float64)


B, N, D, H, DH, GD = 3, 2048, 512, 4, 128, 128
INNER = H * DH
LN_EPS = 1e-5


def silu(v):
    return v / (1.0 + np.exp(-v))


def sigmoid(v):
    return 1.0 / (1.0 + np.exp(-v))


def setup_inputs():
    t = mx_kscale(INNER)
    theta = (10000.0 ** (-2.0 / INNER * np.arange(INNER)) * (1.0 + 0.1 * np.random.standard_normal(INNER))).reshape(H, 1, DH)
    ang = theta * np.arange(N).reshape(1, N, 1)
    tab = np.concatenate([np.cos(ang), np.sin(ang)], axis=-1)
    qs = silu(np.random.standard_normal((B, H, N, DH)))
    mu, m2 = qs.mean(), (qs ** 2).mean()
    kv_mean = mu * mu * tab.sum(1)
    kv_spread = np.sqrt((m2 * m2 - mu ** 4) * (tab ** 2).sum(1))
    kv = (kv_mean[None, :, :, None] + kv_spread[None, :, :, None] * np.random.standard_normal((B, H, 2 * DH, DH))) / np.sqrt(2 * DH)
    return {"q_rot": bf(np.concatenate([qs, qs], axis=-1) * tab[None] / np.sqrt(2 * DH)),
            "kv": bf(kv),
            "g_low": bf(np.random.standard_normal((B, N, GD))),
            "w_g2": bf(np.random.standard_normal((GD, INNER)) / np.sqrt(GD)),
            "ln_gamma": bf((1.0 + 0.1 * np.random.standard_normal(INNER)) * t),
            "ln_beta": bf(0.1 * np.random.standard_normal(INNER) * t),
            "w_out": bf(np.random.standard_normal((INNER, D)) / np.sqrt(INNER) / t[:, None]),
            "b_out": bf(0.1 * np.random.standard_normal(D))}


def reference(q_rot, kv, g_low, w_g2, ln_gamma, ln_beta, w_out, b_out):
    o = f64(q_rot) @ f64(kv)
    o = o.transpose(0, 2, 1, 3).reshape(B, N, INNER)
    mu = o.mean(-1, keepdims=True)
    var = ((o - mu) ** 2).mean(-1, keepdims=True)
    y = (o - mu) / np.sqrt(var + LN_EPS) * f64(ln_gamma) + f64(ln_beta)
    gate = sigmoid(f64(g_low) @ f64(w_g2))
    h = y * gate
    return (mxq(h, 2, "e4m3") @ mxq(f64(w_out), 0, "e4m3")) + f64(b_out)

@@ -1,0 +1,268 @@
+from contextlib import ExitStack
+
+import concourse.mybir as mybir
+from concourse.masks import make_identity
+
+F32 = mybir.dt.float32
+BF16 = mybir.dt.bfloat16
+U32 = mybir.dt.uint32
+U8 = mybir.dt.uint8
+FP8X4 = mybir.dt.float8_e4m3fn_x4
+ACT = mybir.ActivationFunctionType
+ALU = mybir.AluOpType
+
+P = 128
+BATCH, TOKENS, HEADS, QK, DH, GD = 3, 2048, 4, 256, 128, 128
+INNER = HEADS * DH
+D_OUT = 512
+LN_EPS = 1e-5
+PACK = 4
+PAIR = 2
+RUN = 4
+
+TILES_PER_BATCH = TOKENS // P
+TILES = BATCH * TILES_PER_BATCH
+GROUP = 4
+OUT_BUFS = 16
+
+FLOPS = 2 * BATCH * TOKENS * (HEADS * QK * DH + GD * INNER + INNER * D_OUT)
+
+
+def tile_linearattention_pb_t_kernel(
+    tc, q_rot, kv, g_low, w_g2, ln_gamma, ln_beta, w_out, b_out, out
+):
+    nc = tc.nc
+    with ExitStack() as ctx:
+        const = ctx.enter_context(tc.tile_pool(name="const", bufs=1))
+        q_pool = ctx.enter_context(tc.tile_pool(name="q_pool", bufs=TILES))
+        g_pool = ctx.enter_context(tc.tile_pool(name="g_pool", bufs=TILES // GROUP))
+        work2 = ctx.enter_context(tc.tile_pool(name="work2", bufs=2))
+        work3 = ctx.enter_context(tc.tile_pool(name="work3", bufs=3))
+        out_pool = ctx.enter_context(tc.tile_pool(name="out_pool", bufs=OUT_BUFS))
+        psum1 = ctx.enter_context(tc.psum_pool(name="psum1", bufs=1))
+        psum3 = ctx.enter_context(tc.psum_pool(name="psum3", bufs=3))
+
+        def place(i):
+            b, n = divmod(i, TILES_PER_BATCH)
+            return b, n * P
+
+        q_sb = []
+        g_sb = []
+        kv_sb = const.tile([P, BATCH, HEADS, PAIR, DH], BF16)
+        w_g2_raw = const.tile([P, INNER], BF16)
+        ln_raw = const.tile([P, 2, 16], BF16)
+        w_raw = const.tile([P, PACK, D_OUT], BF16)
+        bias_bc = const.tile([P, D_OUT], BF16)
+
+        nc.sync.dma_start(out=ln_raw[:, 0, 0:PACK], in_=ln_gamma.rearrange("(p t) -> p t", t=PACK))
+        nc.sync.dma_start(out=ln_raw[:, 1, 0:PACK], in_=ln_beta.rearrange("(p t) -> p t", t=PACK))
+        for i in range(TILES):
+            b, r = place(i)
+            q_tile = q_pool.tile([P, HEADS, QK], BF16, name="q_tile")
+            nc.sync.dma_start(
+                out=q_tile[:], in_=q_rot[b, :, r : r + P, :].rearrange("h p k -> p h k")
+            )
+            q_sb.append(q_tile)
+            if i % TILES_PER_BATCH == 0:
+                nc.sync.dma_start(
+                    out=kv_sb[:, b].rearrange("w h e d -> w h (e d)"),
+                    in_=kv[b].rearrange("h (w e) d -> w h (e d)", e=PAIR),
+                )
+            if i % GROUP == 0:
+                g_group = g_pool.tile([P, GROUP, GD], BF16, name="g_group")
+                nc.sync.dma_start(
+                    out=g_group[:],
+                    in_=g_low[b, r : r + GROUP * P, :].rearrange("(j p) k -> p j k", p=P),
+                )
+                g_sb.append(g_group)
+            if i == 0:
+                nc.sync.dma_start(out=w_g2_raw[:], in_=w_g2)
+            if i == 1:
+                nc.sync.dma_start(out=w_raw[:], in_=w_out.rearrange("(p t) n -> p t n", t=PACK))
+                nc.sync.dma_start(out=bias_bc[:], in_=b_out.partition_broadcast(P))
+
+        ident_f32 = const.tile([P, P], F32)
+        make_identity(nc, ident_f32[:])
+        ident_bf16 = const.tile([P, P], BF16)
+        make_identity(nc, ident_bf16[:])
+        neg_half = const.tile([P, 1], F32)
+        nc.vector.memset(neg_half[:], -0.5)
+        ln_cols = const.tile([P, 2, PACK], F32)
+        w_g2_sb = const.tile([P, PACK, P], BF16)
+        w_grouped = const.tile([P, D_OUT, PACK], BF16, align_bytes=64)
+        w_codes = const.tile([P, D_OUT], U32, align_bytes=64)
+        w_scales = const.tile([P, D_OUT], U8, align_bytes=64)
+
+        def order_gate_constants():
+            nc.vector.tensor_copy(out=ln_cols[:], in_=ln_raw[:, :, 0:PACK])
+            nc.vector.tensor_copy(
+                out=w_g2_sb[:], in_=w_g2_raw[:].rearrange("c (p t) -> c t p", t=PACK)
+            )
+
+        def quantise_w_out():
+            nc.vector.tensor_copy(out=w_grouped[:], in_=w_raw[:].rearrange("p t n -> p n t"))
+            nc.vector.quantize_mx(
+                out=w_codes[:].bitcast(FP8X4),
+                scales=w_scales[:],
+                in_=w_grouped[:].rearrange("p n t -> p (n t)"),
+            )
+
+        gT_sb, qT_sb, o_ps, stats, mean_var, rstd, shift = {}, {}, {}, {}, {}, {}, {}
+        z_sb, y_sb, gate_sb, h_sb, h_codes, h_scales, out_ps = {}, {}, {}, {}, {}, {}, {}
+
+        def on_scalar(i):
+            return i % 2 == 1
+
+        def transpose_g(group):
+            gT_ps = psum1.tile([P, GROUP * P], BF16, name="gT_ps")
+            for j in range(GROUP):
+                nc.tensor.transpose(gT_ps[:, j * P : (j + 1) * P], g_sb[group][:, j, :], ident_bf16[:])
+            gT_sb[group] = work2.tile([P, GROUP * P], BF16, name="gT")
+            nc.scalar.copy(out=gT_sb[group][:], in_=gT_ps[:])
+
+        def transpose_q(i):
+            q_words = q_sb[i][:].bitcast(F32)
+            qT_ps = psum1.tile([P, HEADS * P], F32, name="qT_ps")
+            for h in range(HEADS):
+                nc.tensor.transpose(qT_ps[:, h * P : (h + 1) * P], q_words[:, h, :], ident_f32[:])
+            qT_sb[i] = work2.tile([P, HEADS * P * PAIR], BF16, name="qT")
+            nc.scalar.copy(out=qT_sb[i][:], in_=qT_ps[:].bitcast(BF16))
+
+        def attend(i):
+            b, r = place(i)
+            o_ps[i] = psum3.tile([P, INNER], F32, name="o_ps")
+            for h in range(HEADS):
+                q_head = qT_sb[i][:, h * P * PAIR : (h + 1) * P * PAIR].rearrange(
+                    "w (n e) -> w n e", e=PAIR
+                )
+                for e in range(PAIR):
+                    nc.tensor.matmul(
+                        o_ps[i][:, h * DH : (h + 1) * DH],
+                        lhsT=q_head[:, :, e],
+                        rhs=kv_sb[:, b, h, e, :],
+                        start=(e == 0),
+                        stop=(e == PAIR - 1),
+                    )
+
+        def partial_statistics(i):
+            stats[i] = work3.tile([P, 6], F32, name="stats")
+            nc.vector.bn_stats(out=stats[i][:], in_=o_ps[i][:])
+
+        def statistics(i):
+            mean_var[i] = work3.tile([P, 2], F32, name="mean_var")
+            nc.vector.bn_aggr(out=mean_var[i][:], in_=stats[i][:])
+
+        def inverse_std(i):
+            var_eps = work3.tile([P, 1], F32, name="var_eps")
+            nc.gpsimd.tensor_scalar(
+                out=var_eps[:], in0=mean_var[i][:, 1:2], scalar1=LN_EPS, scalar2=1.0,
+                op0=ALU.add, op1=ALU.mult,
+            )
+            rstd[i] = work3.tile([P, 1], F32, name="rstd")
+            nc.gpsimd.tensor_tensor(out=rstd[i][:], in0=var_eps[:], in1=neg_half[:], op=ALU.pow)
+            if on_scalar(i):
+                shift[i] = work3.tile([P, 1], F32, name="shift")
+                nc.gpsimd.tensor_scalar(
+                    out=shift[i][:], in0=mean_var[i][:, 0:1], scalar1=rstd[i][:], scalar2=-1.0,
+                    op0=ALU.mult, op1=ALU.mult,
+                )
+
+        def normalise(i):
+            z_sb[i] = work2.tile([P, PACK, P], F32, name="z")
+            o_by_t = o_ps[i][:].rearrange("n (p t) -> n t p", t=PACK)
+            if on_scalar(i):
+                nc.scalar.activation(
+                    out=z_sb[i][:], in_=o_by_t, func=ACT.Identity,
+                    scale=rstd[i][:], bias=shift[i][:],
+                )
+            else:
+                nc.vector.tensor_scalar(
+                    out=z_sb[i][:], in0=o_by_t, scalar1=mean_var[i][:, 0:1], scalar2=rstd[i][:],
+                    op0=ALU.subtract, op1=ALU.mult,
+                )
+
+        def scale_and_shift(i):
+            zT_ps = psum1.tile([P, PACK, P], F32, name="zT_ps")
+            for t in range(PACK):
+                nc.tensor.transpose(zT_ps[:, t, :], z_sb[i][:, t, :], ident_f32[:])
+            y_sb[i] = work2.tile([P, PACK, P], F32, name="y")
+            for t in range(PACK):
+                nc.scalar.activation(
+                    out=y_sb[i][:, t, :], in_=zT_ps[:, t, :], func=ACT.Identity,
+                    scale=ln_cols[:, 0, t : t + 1], bias=ln_cols[:, 1, t : t + 1],
+                )
+
+        def gate(i):
+            group, j = divmod(i, GROUP)
+            gate_ps = psum1.tile([P, PACK, P], F32, name="gate_ps")
+            for t in range(PACK):
+                nc.tensor.matmul(
+                    gate_ps[:, t, :],
+                    lhsT=w_g2_sb[:, t, :],
+                    rhs=gT_sb[group][:, j * P : (j + 1) * P],
+                    start=True,
+                    stop=True,
+                )
+            gate_sb[i] = work3.tile([P, PACK, P], F32, name="gate_sb")
+            nc.scalar.activation(out=gate_sb[i][:], in_=gate_ps[:], func=ACT.Sigmoid)
+
+        def apply_gate(i):
+            h_sb[i] = work2.tile([P, P, PACK], BF16, name="h", align_bytes=64)
+            nc.vector.tensor_tensor(
+                out=h_sb[i][:].rearrange("p (c r) t -> p c t r", r=RUN),
+                in0=y_sb[i][:].rearrange("p t (c r) -> p c t r", r=RUN),
+                in1=gate_sb[i][:].rearrange("p t (c r) -> p c t r", r=RUN),
+                op=ALU.mult,
+            )
+
+        def quantise(i):
+            h_codes[i] = work2.tile([P, P], U32, name="h_codes", align_bytes=64)
+            h_scales[i] = work2.tile([P, P], U8, name="h_scales", align_bytes=64)
+            nc.vector.quantize_mx(
+                out=h_codes[i][:].bitcast(FP8X4),
+                scales=h_scales[i][:],
+                in_=h_sb[i][:].rearrange("p n t -> p (n t)"),
+            )
+
+        def project(i):
+            out_ps[i] = psum1.tile([P, D_OUT], F32, name="out_ps")
+            nc.tensor.matmul_mx(
+                out=out_ps[i][:],
+                lhsT=h_codes[i][:].bitcast(FP8X4),
+                lhsT_scale=h_scales[i][:],
+                rhs=w_codes[:].bitcast(FP8X4),
+                rhs_scale=w_scales[:],
+                start=True,
+                stop=True,
+            )
+
+        def add_bias_and_store(i):
+            b, r = place(i)
+            out_sb = out_pool.tile([P, D_OUT], F32, name="out_sb")
+            nc.vector.tensor_tensor(out=out_sb[:], in0=out_ps[i][:], in1=bias_bc[:], op=ALU.add)
+            nc.sync.dma_start(out=out[b, r : r + P, :], in_=out_sb[:])
+
+        def run(stage, i):
+            if 0 <= i < TILES:
+                stage(i)
+
+        with tc.manual_schedule():
+            for s in range(TILES + 5):
+                if s == 2:
+                    order_gate_constants()
+                if s == 3:
+                    quantise_w_out()
+                if s < TILES and s % GROUP == 0:
+                    transpose_g(s // GROUP)
+                run(transpose_q, s)
+                run(attend, s - 1)
+                run(partial_statistics, s - 1)
+                run(apply_gate, s - 4)
+                run(scale_and_shift, s - 3)
+                run(inverse_std, s - 2)
+                run(statistics, s - 1)
+                run(normalise, s - 2)
+                run(gate, s - 2)
+                run(project, s - 5)
+                run(quantise, s - 4)
+                run(add_bias_and_store, s - 5)

@@ -54,8 +54,6 @@ def tile_linearattention_pb_t_kernel(
         w_raw = const.tile([P, PACK, D_OUT], BF16)
         bias_bc = const.tile([P, D_OUT], BF16)
 
-        nc.sync.dma_start(out=ln_raw[:, 0, 0:PACK], in_=ln_gamma.rearrange("(p t) -> p t", t=PACK))
-        nc.sync.dma_start(out=ln_raw[:, 1, 0:PACK], in_=ln_beta.rearrange("(p t) -> p t", t=PACK))
         for i in range(TILES):
             b, r = place(i)
             q_tile = q_pool.tile([P, HEADS, QK], BF16, name="q_tile")
@@ -68,25 +66,36 @@ def tile_linearattention_pb_t_kernel(
                     out=kv_sb[:, b].rearrange("w h e d -> w h (e d)"),
                     in_=kv[b].rearrange("h (w e) d -> w h (e d)", e=PAIR),
                 )
-            if i % GROUP == 0:
+            if (i == 1) if i < GROUP else (i % GROUP == 0):
+                b, r = place(i - i % GROUP)
                 g_group = g_pool.tile([P, GROUP, GD], BF16, name="g_group")
                 nc.sync.dma_start(
                     out=g_group[:],
                     in_=g_low[b, r : r + GROUP * P, :].rearrange("(j p) k -> p j k", p=P),
                 )
                 g_sb.append(g_group)
-            if i == 0:
-                nc.sync.dma_start(out=w_g2_raw[:], in_=w_g2)
             if i == 1:
+                nc.sync.dma_start(out=w_g2_raw[:], in_=w_g2)
+                nc.sync.dma_start(
+                    out=ln_raw[:, 0, 0:PACK], in_=ln_gamma.rearrange("(p t) -> p t", t=PACK)
+                )
+                nc.sync.dma_start(
+                    out=ln_raw[:, 1, 0:PACK], in_=ln_beta.rearrange("(p t) -> p t", t=PACK)
+                )
+            if i == 2:
                 nc.sync.dma_start(out=w_raw[:], in_=w_out.rearrange("(p t) n -> p t n", t=PACK))
                 nc.sync.dma_start(out=bias_bc[:], in_=b_out.partition_broadcast(P))
 
+        zeros = const.tile([P, D_OUT], BF16)
+        nc.vector.memset(zeros[:], 0.0)
+        neg_half = const.tile([P, 1], F32)
+        nc.vector.memset(neg_half[:], -0.5)
         ident_f32 = const.tile([P, P], F32)
         make_identity(nc, ident_f32[:])
         ident_bf16 = const.tile([P, P], BF16)
         make_identity(nc, ident_bf16[:])
-        neg_half = const.tile([P, 1], F32)
-        nc.vector.memset(neg_half[:], -0.5)
+        table_call = const.tile([P, 1], F32)
+        nc.scalar.activation(out=table_call[:], in_=neg_half[:], func=ACT.Sigmoid)
         ln_cols = const.tile([P, 2, PACK], F32)
         w_g2_sb = const.tile([P, PACK, P], BF16)
         w_grouped = const.tile([P, D_OUT, PACK], BF16, align_bytes=64)
@@ -107,18 +116,25 @@ def tile_linearattention_pb_t_kernel(
                 in_=w_grouped[:].rearrange("p n t -> p (n t)"),
             )
 
+        def keep_tensor_awake(count):
+            for n in range(count):
+                idle_ps = psum1.tile([P, D_OUT], F32, name="out_ps")
+                nc.tensor.matmul(
+                    idle_ps[:], lhsT=zeros[:, 0:P], rhs=zeros[:], start=True, stop=True
+                )
+
         gT_sb, qT_sb, o_ps, stats, mean_var, rstd, shift = {}, {}, {}, {}, {}, {}, {}
         z_sb, y_sb, gate_sb, h_sb, h_codes, h_scales, out_ps = {}, {}, {}, {}, {}, {}, {}
 
         def on_scalar(i):
-            return i % 2 == 1
+            return i % 3 != 0
 
         def transpose_g(group):
             gT_ps = psum1.tile([P, GROUP * P], BF16, name="gT_ps")
             for j in range(GROUP):
                 nc.tensor.transpose(gT_ps[:, j * P : (j + 1) * P], g_sb[group][:, j, :], ident_bf16[:])
             gT_sb[group] = work2.tile([P, GROUP * P], BF16, name="gT")
-            nc.scalar.copy(out=gT_sb[group][:], in_=gT_ps[:])
+            nc.scalar.copy(out=gT_sb[group][:].bitcast(F32), in_=gT_ps[:].bitcast(F32))
 
         def transpose_q(i):
             q_words = q_sb[i][:].bitcast(F32)
@@ -126,7 +142,7 @@ def tile_linearattention_pb_t_kernel(
             for h in range(HEADS):
                 nc.tensor.transpose(qT_ps[:, h * P : (h + 1) * P], q_words[:, h, :], ident_f32[:])
             qT_sb[i] = work2.tile([P, HEADS * P * PAIR], BF16, name="qT")
-            nc.scalar.copy(out=qT_sb[i][:], in_=qT_ps[:].bitcast(BF16))
+            nc.scalar.copy(out=qT_sb[i][:].bitcast(F32), in_=qT_ps[:])
 
         def attend(i):
             b, r = place(i)
@@ -247,15 +263,18 @@ def tile_linearattention_pb_t_kernel(
                 stage(i)
 
         with tc.manual_schedule():
+            keep_tensor_awake(2)
             for s in range(TILES + 5):
                 if s == 2:
                     order_gate_constants()
                 if s == 3:
                     quantise_w_out()
-                if s < TILES and s % GROUP == 0:
-                    transpose_g(s // GROUP)
                 run(transpose_q, s)
                 run(attend, s - 1)
+                if s < TILES and s % GROUP == 1:
+                    transpose_g(s // GROUP)
+                if s < 5:
+                    keep_tensor_awake(1)
                 run(partial_statistics, s - 1)
                 run(apply_gate, s - 4)
                 run(scale_and_shift, s - 3)

@@ -66,6 +66,8 @@ def tile_linearattention_pb_t_kernel(
                     out=kv_sb[:, b].rearrange("w h e d -> w h (e d)"),
                     in_=kv[b].rearrange("h (w e) d -> w h (e d)", e=PAIR),
                 )
+            if i == 1:
+                nc.sync.dma_start(out=w_raw[:], in_=w_out.rearrange("(p t) n -> p t n", t=PACK))
             if (i == 1) if i < GROUP else (i % GROUP == 0):
                 b, r = place(i - i % GROUP)
                 g_group = g_pool.tile([P, GROUP, GD], BF16, name="g_group")
@@ -83,7 +85,6 @@ def tile_linearattention_pb_t_kernel(
                     out=ln_raw[:, 1, 0:PACK], in_=ln_beta.rearrange("(p t) -> p t", t=PACK)
                 )
             if i == 2:
-                nc.sync.dma_start(out=w_raw[:], in_=w_out.rearrange("(p t) n -> p t n", t=PACK))
                 nc.sync.dma_start(out=bias_bc[:], in_=b_out.partition_broadcast(P))
 
         zeros = const.tile([P, D_OUT], BF16)
@@ -108,8 +109,10 @@ def tile_linearattention_pb_t_kernel(
                 out=w_g2_sb[:], in_=w_g2_raw[:].rearrange("c (p t) -> c t p", t=PACK)
             )
 
-        def quantise_w_out():
+        def interleave_w_out():
             nc.vector.tensor_copy(out=w_grouped[:], in_=w_raw[:].rearrange("p t n -> p n t"))
+
+        def quantise_w_out():
             nc.vector.quantize_mx(
                 out=w_codes[:].bitcast(FP8X4),
                 scales=w_scales[:],
@@ -127,7 +130,7 @@ def tile_linearattention_pb_t_kernel(
         z_sb, y_sb, gate_sb, h_sb, h_codes, h_scales, out_ps = {}, {}, {}, {}, {}, {}, {}
 
         def on_scalar(i):
-            return i % 3 != 0
+            return i >= 4 and i % 5 not in (1, 3)
 
         def transpose_g(group):
             gT_ps = psum1.tile([P, GROUP * P], BF16, name="gT_ps")
@@ -263,12 +266,10 @@ def tile_linearattention_pb_t_kernel(
                 stage(i)
 
         with tc.manual_schedule():
-            keep_tensor_awake(2)
+            keep_tensor_awake(3)
             for s in range(TILES + 5):
-                if s == 2:
-                    order_gate_constants()
-                if s == 3:
-                    quantise_w_out()
+                if s == 1:
+                    interleave_w_out()
                 run(transpose_q, s)
                 run(attend, s - 1)
                 if s < TILES and s % GROUP == 1:
@@ -280,6 +281,9 @@ def tile_linearattention_pb_t_kernel(
                 run(scale_and_shift, s - 3)
                 run(inverse_std, s - 2)
                 run(statistics, s - 1)
+                if s == 1:
+                    order_gate_constants()
+                    quantise_w_out()
                 run(normalise, s - 2)
                 run(gate, s - 2)
                 run(project, s - 5)

@@ -23,7 +23,7 @@ RUN = 4
 TILES_PER_BATCH = TOKENS // P
 TILES = BATCH * TILES_PER_BATCH
 GROUP = 4
-OUT_BUFS = 16
+Q_BUFS = 32
 
 FLOPS = 2 * BATCH * TOKENS * (HEADS * QK * DH + GD * INNER + INNER * D_OUT)
 
@@ -34,11 +34,12 @@ def tile_linearattention_pb_t_kernel(
     nc = tc.nc
     with ExitStack() as ctx:
         const = ctx.enter_context(tc.tile_pool(name="const", bufs=1))
-        q_pool = ctx.enter_context(tc.tile_pool(name="q_pool", bufs=TILES))
+        q_pool = ctx.enter_context(tc.tile_pool(name="q_pool", bufs=Q_BUFS))
         g_pool = ctx.enter_context(tc.tile_pool(name="g_pool", bufs=TILES // GROUP))
         work2 = ctx.enter_context(tc.tile_pool(name="work2", bufs=2))
         work3 = ctx.enter_context(tc.tile_pool(name="work3", bufs=3))
-        out_pool = ctx.enter_context(tc.tile_pool(name="out_pool", bufs=OUT_BUFS))
+        work4 = ctx.enter_context(tc.tile_pool(name="work4", bufs=4))
+        out_pool = ctx.enter_context(tc.tile_pool(name="out_pool", bufs=TILES))
         psum1 = ctx.enter_context(tc.psum_pool(name="psum1", bufs=1))
         psum3 = ctx.enter_context(tc.psum_pool(name="psum3", bufs=3))
 
@@ -187,7 +188,7 @@ def tile_linearattention_pb_t_kernel(
                 )
 
         def normalise(i):
-            z_sb[i] = work2.tile([P, PACK, P], F32, name="z")
+            z_sb[i] = work3.tile([P, PACK, P], F32, name="z")
             o_by_t = o_ps[i][:].rearrange("n (p t) -> n t p", t=PACK)
             if on_scalar(i):
                 nc.scalar.activation(
@@ -204,7 +205,7 @@ def tile_linearattention_pb_t_kernel(
             zT_ps = psum1.tile([P, PACK, P], F32, name="zT_ps")
             for t in range(PACK):
                 nc.tensor.transpose(zT_ps[:, t, :], z_sb[i][:, t, :], ident_f32[:])
-            y_sb[i] = work2.tile([P, PACK, P], F32, name="y")
+            y_sb[i] = work3.tile([P, PACK, P], F32, name="y")
             for t in range(PACK):
                 nc.scalar.activation(
                     out=y_sb[i][:, t, :], in_=zT_ps[:, t, :], func=ACT.Identity,
@@ -222,7 +223,7 @@ def tile_linearattention_pb_t_kernel(
                     start=True,
                     stop=True,
                 )
-            gate_sb[i] = work3.tile([P, PACK, P], F32, name="gate_sb")
+            gate_sb[i] = work4.tile([P, PACK, P], F32, name="gate_sb")
             nc.scalar.activation(out=gate_sb[i][:], in_=gate_ps[:], func=ACT.Sigmoid)
 
         def apply_gate(i):

from contextlib import ExitStack

import concourse.mybir as mybir
from concourse.masks import make_identity

F32 = mybir.dt.float32
BF16 = mybir.dt.bfloat16
U32 = mybir.dt.uint32
U8 = mybir.dt.uint8
FP8X4 = mybir.dt.float8_e4m3fn_x4
ACT = mybir.ActivationFunctionType
ALU = mybir.AluOpType

P = 128
BATCH, TOKENS, HEADS, QK, DH, GD = 3, 2048, 4, 256, 128, 128
INNER = HEADS * DH
D_OUT = 512
LN_EPS = 1e-5
PACK = 4
PAIR = 2
RUN = 4

TILES_PER_BATCH = TOKENS // P
TILES = BATCH * TILES_PER_BATCH
GROUP = 4
Q_BUFS = 32

FLOPS = 2 * BATCH * TOKENS * (HEADS * QK * DH + GD * INNER + INNER * D_OUT)


def tile_linearattention_pb_t_kernel(
    tc, q_rot, kv, g_low, w_g2, ln_gamma, ln_beta, w_out, b_out, out
):
    nc = tc.nc
    with ExitStack() as ctx:
        const = ctx.enter_context(tc.tile_pool(name="const", bufs=1))
        q_pool = ctx.enter_context(tc.tile_pool(name="q_pool", bufs=Q_BUFS))
        g_pool = ctx.enter_context(tc.tile_pool(name="g_pool", bufs=TILES // GROUP))
        work2 = ctx.enter_context(tc.tile_pool(name="work2", bufs=2))
        work3 = ctx.enter_context(tc.tile_pool(name="work3", bufs=3))
        work4 = ctx.enter_context(tc.tile_pool(name="work4", bufs=4))
        out_pool = ctx.enter_context(tc.tile_pool(name="out_pool", bufs=TILES))
        psum1 = ctx.enter_context(tc.psum_pool(name="psum1", bufs=1))
        psum3 = ctx.enter_context(tc.psum_pool(name="psum3", bufs=3))

        def place(i):
            b, n = divmod(i, TILES_PER_BATCH)
            return b, n * P

        q_sb = []
        g_sb = []
        kv_sb = const.tile([P, BATCH, HEADS, PAIR, DH], BF16)
        w_g2_raw = const.tile([P, INNER], BF16)
        ln_raw = const.tile([P, 2, 16], BF16)
        w_raw = const.tile([P, PACK, D_OUT], BF16)
        bias_bc = const.tile([P, D_OUT], BF16)

        for i in range(TILES):
            b, r = place(i)
            q_tile = q_pool.tile([P, HEADS, QK], BF16, name="q_tile")
            nc.sync.dma_start(
                out=q_tile[:], in_=q_rot[b, :, r : r + P, :].rearrange("h p k -> p h k")
            )
            q_sb.append(q_tile)
            if i % TILES_PER_BATCH == 0:
                nc.sync.dma_start(
                    out=kv_sb[:, b].rearrange("w h e d -> w h (e d)"),
                    in_=kv[b].rearrange("h (w e) d -> w h (e d)", e=PAIR),
                )
            if i == 1:
                nc.sync.dma_start(out=w_raw[:], in_=w_out.rearrange("(p t) n -> p t n", t=PACK))
            if (i == 1) if i < GROUP else (i % GROUP == 0):
                b, r = place(i - i % GROUP)
                g_group = g_pool.tile([P, GROUP, GD], BF16, name="g_group")
                nc.sync.dma_start(
                    out=g_group[:],
                    in_=g_low[b, r : r + GROUP * P, :].rearrange("(j p) k -> p j k", p=P),
                )
                g_sb.append(g_group)
            if i == 1:
                nc.sync.dma_start(out=w_g2_raw[:], in_=w_g2)
                nc.sync.dma_start(
                    out=ln_raw[:, 0, 0:PACK], in_=ln_gamma.rearrange("(p t) -> p t", t=PACK)
                )
                nc.sync.dma_start(
                    out=ln_raw[:, 1, 0:PACK], in_=ln_beta.rearrange("(p t) -> p t", t=PACK)
                )
            if i == 2:
                nc.sync.dma_start(out=bias_bc[:], in_=b_out.partition_broadcast(P))

        zeros = const.tile([P, D_OUT], BF16)
        nc.vector.memset(zeros[:], 0.0)
        neg_half = const.tile([P, 1], F32)
        nc.vector.memset(neg_half[:], -0.5)
        ident_f32 = const.tile([P, P], F32)
        make_identity(nc, ident_f32[:])
        ident_bf16 = const.tile([P, P], BF16)
        make_identity(nc, ident_bf16[:])
        table_call = const.tile([P, 1], F32)
        nc.scalar.activation(out=table_call[:], in_=neg_half[:], func=ACT.Sigmoid)
        ln_cols = const.tile([P, 2, PACK], F32)
        w_g2_sb = const.tile([P, PACK, P], BF16)
        w_grouped = const.tile([P, D_OUT, PACK], BF16, align_bytes=64)
        w_codes = const.tile([P, D_OUT], U32, align_bytes=64)
        w_scales = const.tile([P, D_OUT], U8, align_bytes=64)

        def order_gate_constants():
            nc.vector.tensor_copy(out=ln_cols[:], in_=ln_raw[:, :, 0:PACK])
            nc.vector.tensor_copy(
                out=w_g2_sb[:], in_=w_g2_raw[:].rearrange("c (p t) -> c t p", t=PACK)
            )

        def interleave_w_out():
            nc.vector.tensor_copy(out=w_grouped[:], in_=w_raw[:].rearrange("p t n -> p n t"))

        def quantise_w_out():
            nc.vector.quantize_mx(
                out=w_codes[:].bitcast(FP8X4),
                scales=w_scales[:],
                in_=w_grouped[:].rearrange("p n t -> p (n t)"),
            )

        def keep_tensor_awake(count):
            for n in range(count):
                idle_ps = psum1.tile([P, D_OUT], F32, name="out_ps")
                nc.tensor.matmul(
                    idle_ps[:], lhsT=zeros[:, 0:P], rhs=zeros[:], start=True, stop=True
                )

        gT_sb, qT_sb, o_ps, stats, mean_var, rstd, shift = {}, {}, {}, {}, {}, {}, {}
        z_sb, y_sb, gate_sb, h_sb, h_codes, h_scales, out_ps = {}, {}, {}, {}, {}, {}, {}

        def on_scalar(i):
            return i >= 4 and i % 5 not in (1, 3)

        def transpose_g(group):
            gT_ps = psum1.tile([P, GROUP * P], BF16, name="gT_ps")
            for j in range(GROUP):
                nc.tensor.transpose(gT_ps[:, j * P : (j + 1) * P], g_sb[group][:, j, :], ident_bf16[:])
            gT_sb[group] = work2.tile([P, GROUP * P], BF16, name="gT")
            nc.scalar.copy(out=gT_sb[group][:].bitcast(F32), in_=gT_ps[:].bitcast(F32))

        def transpose_q(i):
            q_words = q_sb[i][:].bitcast(F32)
            qT_ps = psum1.tile([P, HEADS * P], F32, name="qT_ps")
            for h in range(HEADS):
                nc.tensor.transpose(qT_ps[:, h * P : (h + 1) * P], q_words[:, h, :], ident_f32[:])
            qT_sb[i] = work2.tile([P, HEADS * P * PAIR], BF16, name="qT")
            nc.scalar.copy(out=qT_sb[i][:].bitcast(F32), in_=qT_ps[:])

        def attend(i):
            b, r = place(i)
            o_ps[i] = psum3.tile([P, INNER], F32, name="o_ps")
            for h in range(HEADS):
                q_head = qT_sb[i][:, h * P * PAIR : (h + 1) * P * PAIR].rearrange(
                    "w (n e) -> w n e", e=PAIR
                )
                for e in range(PAIR):
                    nc.tensor.matmul(
                        o_ps[i][:, h * DH : (h + 1) * DH],
                        lhsT=q_head[:, :, e],
                        rhs=kv_sb[:, b, h, e, :],
                        start=(e == 0),
                        stop=(e == PAIR - 1),
                    )

        def partial_statistics(i):
            stats[i] = work3.tile([P, 6], F32, name="stats")
            nc.vector.bn_stats(out=stats[i][:], in_=o_ps[i][:])

        def statistics(i):
            mean_var[i] = work3.tile([P, 2], F32, name="mean_var")
            nc.vector.bn_aggr(out=mean_var[i][:], in_=stats[i][:])

        def inverse_std(i):
            var_eps = work3.tile([P, 1], F32, name="var_eps")
            nc.gpsimd.tensor_scalar(
                out=var_eps[:], in0=mean_var[i][:, 1:2], scalar1=LN_EPS, scalar2=1.0,
                op0=ALU.add, op1=ALU.mult,
            )
            rstd[i] = work3.tile([P, 1], F32, name="rstd")
            nc.gpsimd.tensor_tensor(out=rstd[i][:], in0=var_eps[:], in1=neg_half[:], op=ALU.pow)
            if on_scalar(i):
                shift[i] = work3.tile([P, 1], F32, name="shift")
                nc.gpsimd.tensor_scalar(
                    out=shift[i][:], in0=mean_var[i][:, 0:1], scalar1=rstd[i][:], scalar2=-1.0,
                    op0=ALU.mult, op1=ALU.mult,
                )

        def normalise(i):
            z_sb[i] = work3.tile([P, PACK, P], F32, name="z")
            o_by_t = o_ps[i][:].rearrange("n (p t) -> n t p", t=PACK)
            if on_scalar(i):
                nc.scalar.activation(
                    out=z_sb[i][:], in_=o_by_t, func=ACT.Identity,
                    scale=rstd[i][:], bias=shift[i][:],
                )
            else:
                nc.vector.tensor_scalar(
                    out=z_sb[i][:], in0=o_by_t, scalar1=mean_var[i][:, 0:1], scalar2=rstd[i][:],
                    op0=ALU.subtract, op1=ALU.mult,
                )

        def scale_and_shift(i):
            zT_ps = psum1.tile([P, PACK, P], F32, name="zT_ps")
            for t in range(PACK):
                nc.tensor.transpose(zT_ps[:, t, :], z_sb[i][:, t, :], ident_f32[:])
            y_sb[i] = work3.tile([P, PACK, P], F32, name="y")
            for t in range(PACK):
                nc.scalar.activation(
                    out=y_sb[i][:, t, :], in_=zT_ps[:, t, :], func=ACT.Identity,
                    scale=ln_cols[:, 0, t : t + 1], bias=ln_cols[:, 1, t : t + 1],
                )

        def gate(i):
            group, j = divmod(i, GROUP)
            gate_ps = psum1.tile([P, PACK, P], F32, name="gate_ps")
            for t in range(PACK):
                nc.tensor.matmul(
                    gate_ps[:, t, :],
                    lhsT=w_g2_sb[:, t, :],
                    rhs=gT_sb[group][:, j * P : (j + 1) * P],
                    start=True,
                    stop=True,
                )
            gate_sb[i] = work4.tile([P, PACK, P], F32, name="gate_sb")
            nc.scalar.activation(out=gate_sb[i][:], in_=gate_ps[:], func=ACT.Sigmoid)

        def apply_gate(i):
            h_sb[i] = work2.tile([P, P, PACK], BF16, name="h", align_bytes=64)
            nc.vector.tensor_tensor(
                out=h_sb[i][:].rearrange("p (c r) t -> p c t r", r=RUN),
                in0=y_sb[i][:].rearrange("p t (c r) -> p c t r", r=RUN),
                in1=gate_sb[i][:].rearrange("p t (c r) -> p c t r", r=RUN),
                op=ALU.mult,
            )

        def quantise(i):
            h_codes[i] = work2.tile([P, P], U32, name="h_codes", align_bytes=64)
            h_scales[i] = work2.tile([P, P], U8, name="h_scales", align_bytes=64)
            nc.vector.quantize_mx(
                out=h_codes[i][:].bitcast(FP8X4),
                scales=h_scales[i][:],
                in_=h_sb[i][:].rearrange("p n t -> p (n t)"),
            )

        def project(i):
            out_ps[i] = psum1.tile([P, D_OUT], F32, name="out_ps")
            nc.tensor.matmul_mx(
                out=out_ps[i][:],
                lhsT=h_codes[i][:].bitcast(FP8X4),
                lhsT_scale=h_scales[i][:],
                rhs=w_codes[:].bitcast(FP8X4),
                rhs_scale=w_scales[:],
                start=True,
                stop=True,
            )

        def add_bias_and_store(i):
            b, r = place(i)
            out_sb = out_pool.tile([P, D_OUT], F32, name="out_sb")
            nc.vector.tensor_tensor(out=out_sb[:], in0=out_ps[i][:], in1=bias_bc[:], op=ALU.add)
            nc.sync.dma_start(out=out[b, r : r + P, :], in_=out_sb[:])

        def run(stage, i):
            if 0 <= i < TILES:
                stage(i)

        with tc.manual_schedule():
            keep_tensor_awake(3)
            for s in range(TILES + 5):
                if s == 1:
                    interleave_w_out()
                run(transpose_q, s)
                run(attend, s - 1)
                if s < TILES and s % GROUP == 1:
                    transpose_g(s // GROUP)
                if s < 5:
                    keep_tensor_awake(1)
                run(partial_statistics, s - 1)
                run(apply_gate, s - 4)
                run(scale_and_shift, s - 3)
                run(inverse_std, s - 2)
                run(statistics, s - 1)
                if s == 1:
                    order_gate_constants()
                    quantise_w_out()
                run(normalise, s - 2)
                run(gate, s - 2)
                run(project, s - 5)
                run(quantise, s - 4)
                run(add_bias_and_store, s - 5)
